import numpy as np
import ml_dtypes


def mxq(x, axis, fmt="e4m3"):
    dtype, down = {"e4m3": (ml_dtypes.float8_e4m3fn, 7), "e5m2": (ml_dtypes.float8_e5m2, 14)}[fmt]
    v = np.moveaxis(np.asarray(x, np.float32).astype(ml_dtypes.bfloat16).astype(np.float64), axis, -1)
    blocks = v.reshape(v.shape[:-1] + (-1, 32))
    amax = np.abs(blocks).max(-1, keepdims=True)
    byte = np.maximum(np.where(amax > 0, np.frexp(amax)[1] - 1 + 127, 0) - down, 1)
    scale = np.exp2(byte - 127.0)
    codes = (blocks / scale).astype(np.float32).astype(dtype).astype(np.float64)
    return np.moveaxis((codes * scale).reshape(v.shape), -1, axis)


WIDE = False


def mx_kscale(k):
    if not WIDE:
        return np.ones(k)
    levels = np.array([10, -10, 5, -5, 0])
    a = np.random.permutation(np.resize(levels, k // 512 * 4)).reshape(k // 512, 4)
    idx = np.arange(k)
    return np.exp2(a[idx // 512, idx % 128 // 32])


BF16 = ml_dtypes.bfloat16


def bf(x):
    return np.asarray(x, np.float32).astype(BF16)


def f64(x):
    return np.asarray(x).astype(np.float64)


N, NQ, G, KW = 1536, 512, 3, 3
P = KW - 1


def x_taps(x):
    return np.moveaxis(x.reshape(N, NQ, G, P), -1, 0).swapaxes(-1, -2).reshape(P, N * G, NQ)


def q_rows(q):
    return q.swapaxes(-1, -2).reshape(N * G, NQ)


def conv(xq, qq, W, b):
    wt = W.transpose(2, 1, 0)
    return (xq @ mxq(wt[:P], 1, "e4m3")).sum(0) + (qq @ mxq(wt[P], 0, "e4m3")) + b


def setup_inputs():
    s = mx_kscale(NQ)
    w = 1.0 / np.sqrt(KW * NQ)
    return {"x": bf(np.random.standard_normal((N, NQ, G * P)) * s[None, :, None]),
            "q2": bf(np.maximum(np.random.standard_normal((N, NQ, G)) * 0.9, 0.0) * s[None, :, None]),
            "q1": bf(np.random.standard_normal((N, NQ, G))),
            "W3": bf(np.random.standard_normal((NQ, NQ, KW)) * w / s[None, :, None]),
            "b3": bf(np.random.standard_normal(NQ) * 0.2)}


def reference(x, q2, q1, W3, b3):
    y = conv(mxq(x_taps(f64(x)), 2, "e4m3"), mxq(q_rows(f64(q2)), 1, "e4m3"), f64(W3), f64(b3))
    return np.maximum(y.reshape(N, G, NQ).swapaxes(-1, -2) + f64(q1), 0.0)

@@ -1,0 +1,143 @@
+from contextlib import ExitStack
+
+import concourse.mybir as mybir
+from concourse.masks import make_identity
+
+F32 = mybir.dt.float32
+BF16 = mybir.dt.bfloat16
+U32 = mybir.dt.uint32
+U8 = mybir.dt.uint8
+FP8X4 = mybir.dt.float8_e4m3fn_x4
+ADD = mybir.AluOpType.add
+RELU = mybir.ActivationFunctionType.Relu
+
+P = 128
+N, C, G, KW = 1536, 512, 3, 3
+O = 512
+NT = N // P
+U = C // P
+OT = O // P
+NPOS = 9
+FLOPS = 2 * N * G * O * C * KW
+
+
+def tile_quadjetresnetblock_pb_t_kernel(tc, x, q2, q1, W3, b3, out):
+    nc = tc.nc
+    x_t = x.rearrange("(i p) c j -> i p (c j)", p=P)
+    q2_t = q2.rearrange("(i p) c g -> i p (c g)", p=P)
+    q1_t = q1.rearrange("(i p) c g -> i p (c g)", p=P)
+    out_t = out.rearrange("(i p) o g -> i p (o g)", p=P)
+    w_t = W3.rearrange("(t p) c k -> t p (c k)", p=P)
+
+    with ExitStack() as ctx:
+        const = ctx.enter_context(tc.tile_pool(name="const", bufs=1))
+        xin = ctx.enter_context(tc.tile_pool(name="xin", bufs=4))
+        work = ctx.enter_context(tc.tile_pool(name="work", bufs=2))
+        res = ctx.enter_context(tc.tile_pool(name="res", bufs=4))
+        pst = ctx.enter_context(tc.psum_pool(name="pst", bufs=4))
+        psm = ctx.enter_context(tc.psum_pool(name="psm", bufs=4))
+
+        ident_f = const.tile([P, P], F32)
+        make_identity(nc, ident_f[:])
+        ident_b = const.tile([P, P], BF16)
+        make_identity(nc, ident_b[:])
+
+        b_bc = const.tile([P, O], BF16)
+        nc.scalar.dma_start(out=b_bc[:], in_=b3.partition_broadcast(P))
+
+        w_sb = const.tile([P, OT, C * KW], BF16)
+        for t in range(OT):
+            nc.sync.dma_start(out=w_sb[:, t, :], in_=w_t[t])
+        w_grp = const.tile([P, KW, O, U], BF16, align_bytes=64)
+        w_codes = const.tile([P, KW, O], U32, align_bytes=64)
+        w_scales = const.tile([P, KW, O], U8, align_bytes=64)
+        for t in range(OT):
+            wv = w_sb[:, t, :].rearrange("p (c k) -> p k c", k=KW)
+            for k0, nk in ((0, 2), (2, 1)):
+                wt = pst.tile([P, nk * U * P], BF16, tag="tr")
+                for k in range(nk):
+                    for u in range(U):
+                        j = k * U + u
+                        nc.tensor.transpose(wt[:, j * P:(j + 1) * P], wv[:, k0 + k, u * P:(u + 1) * P], ident_b[:])
+                src = wt[:].rearrange("p (k u o) -> p k o u", k=nk, u=U)
+                dst = w_grp[:, k0:k0 + nk, t * P:(t + 1) * P, :]
+                if nk == 2:
+                    nc.vector.tensor_copy(out=dst, in_=src)
+                else:
+                    nc.scalar.copy(out=dst, in_=src)
+        for k in range(KW):
+            nc.vector.quantize_mx(
+                out=w_codes[:, k, :].bitcast(FP8X4),
+                scales=w_scales[:, k, :],
+                in_=w_grp[:, k, :, :].rearrange("p o u -> p (o u)"),
+            )
+
+        for i in range(NT):
+            x_sb = xin.tile([P, C * 6], BF16)
+            nc.sync.dma_start(out=x_sb[:], in_=x_t[i])
+            q2_sb = xin.tile([P, C * G], BF16)
+            nc.sync.dma_start(out=q2_sb[:], in_=q2_t[i])
+            q1_sb = xin.tile([P, C * G], BF16)
+            nc.sync.dma_start(out=q1_sb[:], in_=q1_t[i])
+
+            grp = work.tile([P, NPOS, P, U], BF16, align_bytes=64)
+            codes = work.tile([P, NPOS, P], U32, align_bytes=64)
+            scales = work.tile([P, NPOS, P], U8, align_bytes=64)
+
+            xw = x_sb[:].bitcast(F32).rearrange("p (c g) -> p g c", g=G)
+            for g in range(G):
+                xt = pst.tile([P, U * P], F32, tag="tr")
+                for u in range(U):
+                    nc.tensor.transpose(xt[:, u * P:(u + 1) * P], xw[:, g, u * P:(u + 1) * P], ident_f[:])
+                nc.scalar.copy(
+                    out=grp[:, 2 * g:2 * g + 2, :, :],
+                    in_=xt[:].bitcast(BF16).rearrange("p (u m t) -> p t m u", u=U, t=2),
+                )
+            qv = q2_sb[:].rearrange("p (c g) -> p g c", g=G)
+            for g0, ng in ((0, 2), (2, 1)):
+                qt = pst.tile([P, ng * U * P], BF16, tag="tr")
+                for g in range(ng):
+                    for u in range(U):
+                        j = g * U + u
+                        nc.tensor.transpose(qt[:, j * P:(j + 1) * P], qv[:, g0 + g, u * P:(u + 1) * P], ident_b[:])
+                nc.vector.tensor_copy(
+                    out=grp[:, 6 + g0:6 + g0 + ng, :, :],
+                    in_=qt[:].rearrange("p (g u m) -> p g m u", g=ng, u=U),
+                )
+            for p0, npos in ((0, 2), (2, 2), (4, 2), (6, 2), (8, 1)):
+                nc.vector.quantize_mx(
+                    out=codes[:, p0:p0 + npos, :].rearrange("p a m -> p (a m)").bitcast(FP8X4),
+                    scales=scales[:, p0:p0 + npos, :].rearrange("p a m -> p (a m)"),
+                    in_=grp[:, p0:p0 + npos, :, :].rearrange("p a m u -> p (a m u)"),
+                )
+
+            acc = res.tile([P, O * G], F32)
+            nc.gpsimd.tensor_tensor(
+                out=acc[:].rearrange("p (o g) -> p o g", g=G),
+                in0=q1_sb[:].rearrange("p (o g) -> p o g", g=G),
+                in1=b_bc[:].unsqueeze(2).to_broadcast([P, O, G]),
+                op=ADD,
+            )
+            for oc in range(OT):
+                ps = psm.tile([P, G, P], F32, tag="mm")
+                for g in range(G):
+                    for k in range(KW):
+                        pos = 2 * g + k if k < 2 else 6 + g
+                        nc.tensor.matmul_mx(
+                            out=ps[:, g, :],
+                            lhsT=codes[:, pos, :].bitcast(FP8X4),
+                            lhsT_scale=scales[:, pos, :],
+                            rhs=w_codes[:, k, oc * P:(oc + 1) * P].bitcast(FP8X4),
+                            rhs_scale=w_scales[:, k, oc * P:(oc + 1) * P],
+                            start=(k == 0),
+                            stop=(k == KW - 1),
+                        )
+                part = acc[:, oc * P * G:(oc + 1) * P * G]
+                nc.vector.tensor_tensor(
+                    out=part.rearrange("p (o g) -> p o g", g=G),
+                    in0=ps[:].rearrange("p g o -> p o g"),
+                    in1=part.rearrange("p (o g) -> p o g", g=G),
+                    op=ADD,
+                )
+            nc.scalar.activation(out=acc[:], in_=acc[:], func=RELU)
+            nc.scalar.dma_start(out=out_t[i], in_=acc[:])

@@ -17,127 +17,193 @@ O = 512
 NT = N // P
 U = C // P
 OT = O // P
+NB = 4
 NPOS = 9
+AHEAD = 2
 FLOPS = 2 * N * G * O * C * KW
 
 
 def tile_quadjetresnetblock_pb_t_kernel(tc, x, q2, q1, W3, b3, out):
     nc = tc.nc
     x_t = x.rearrange("(i p) c j -> i p (c j)", p=P)
-    q2_t = q2.rearrange("(i p) c g -> i p (c g)", p=P)
+    q2_t = q2.rearrange("n (u c) g -> (n u) (c g)", u=U).rearrange("(i b p) f -> i p b f", b=NB, p=P)
     q1_t = q1.rearrange("(i p) c g -> i p (c g)", p=P)
     out_t = out.rearrange("(i p) o g -> i p (o g)", p=P)
-    w_t = W3.rearrange("(t p) c k -> t p (c k)", p=P)
+    w_t = W3.rearrange("o (u c) k -> (o u) (c k)", u=U).rearrange("(h b p) f -> h p b f", h=2, p=P)
 
     with ExitStack() as ctx:
         const = ctx.enter_context(tc.tile_pool(name="const", bufs=1))
-        xin = ctx.enter_context(tc.tile_pool(name="xin", bufs=4))
+        xin = ctx.enter_context(tc.tile_pool(name="xin", bufs=AHEAD + 2))
         work = ctx.enter_context(tc.tile_pool(name="work", bufs=2))
         res = ctx.enter_context(tc.tile_pool(name="res", bufs=4))
         pst = ctx.enter_context(tc.psum_pool(name="pst", bufs=4))
         psm = ctx.enter_context(tc.psum_pool(name="psm", bufs=4))
+        ctx.enter_context(tc.manual_schedule())
 
-        ident_f = const.tile([P, P], F32)
-        make_identity(nc, ident_f[:])
-        ident_b = const.tile([P, P], BF16)
-        make_identity(nc, ident_b[:])
+        x_sb, q2_sb, q1_sb, grp, codes, scales, acc, ps = {}, {}, {}, {}, {}, {}, {}, {}
 
-        b_bc = const.tile([P, O], BF16)
-        nc.scalar.dma_start(out=b_bc[:], in_=b3.partition_broadcast(P))
+        def load(i):
+            x_sb[i] = xin.tile([P, C * 6], BF16, name="x_sb")
+            nc.sync.dma_start(out=x_sb[i][:], in_=x_t[i])
+            q2_sb[i] = xin.tile([P, NB, P * G], BF16, name="q2_sb")
+            nc.sync.dma_start(out=q2_sb[i][:], in_=q2_t[i])
+            q1_sb[i] = xin.tile([P, C * G], BF16, name="q1_sb")
+            nc.sync.dma_start(out=q1_sb[i][:], in_=q1_t[i])
 
-        w_sb = const.tile([P, OT, C * KW], BF16)
-        for t in range(OT):
-            nc.sync.dma_start(out=w_sb[:, t, :], in_=w_t[t])
-        w_grp = const.tile([P, KW, O, U], BF16, align_bytes=64)
-        w_codes = const.tile([P, KW, O], U32, align_bytes=64)
-        w_scales = const.tile([P, KW, O], U8, align_bytes=64)
-        for t in range(OT):
-            wv = w_sb[:, t, :].rearrange("p (c k) -> p k c", k=KW)
-            for k0, nk in ((0, 2), (2, 1)):
-                wt = pst.tile([P, nk * U * P], BF16, tag="tr")
-                for k in range(nk):
-                    for u in range(U):
-                        j = k * U + u
-                        nc.tensor.transpose(wt[:, j * P:(j + 1) * P], wv[:, k0 + k, u * P:(u + 1) * P], ident_b[:])
-                src = wt[:].rearrange("p (k u o) -> p k o u", k=nk, u=U)
-                dst = w_grp[:, k0:k0 + nk, t * P:(t + 1) * P, :]
-                if nk == 2:
-                    nc.vector.tensor_copy(out=dst, in_=src)
-                else:
-                    nc.scalar.copy(out=dst, in_=src)
-        for k in range(KW):
-            nc.vector.quantize_mx(
-                out=w_codes[:, k, :].bitcast(FP8X4),
-                scales=w_scales[:, k, :],
-                in_=w_grp[:, k, :, :].rearrange("p o u -> p (o u)"),
-            )
-
-        for i in range(NT):
-            x_sb = xin.tile([P, C * 6], BF16)
-            nc.sync.dma_start(out=x_sb[:], in_=x_t[i])
-            q2_sb = xin.tile([P, C * G], BF16)
-            nc.sync.dma_start(out=q2_sb[:], in_=q2_t[i])
-            q1_sb = xin.tile([P, C * G], BF16)
-            nc.sync.dma_start(out=q1_sb[:], in_=q1_t[i])
-
-            grp = work.tile([P, NPOS, P, U], BF16, align_bytes=64)
-            codes = work.tile([P, NPOS, P], U32, align_bytes=64)
-            scales = work.tile([P, NPOS, P], U8, align_bytes=64)
-
-            xw = x_sb[:].bitcast(F32).rearrange("p (c g) -> p g c", g=G)
+        def tx_x(i):
+            grp[i] = work.tile([P, NPOS, P, U], BF16, align_bytes=64, name="grp")
+            codes[i] = work.tile([P, NPOS, P], U32, align_bytes=64, name="codes")
+            scales[i] = work.tile([P, NPOS, P], U8, align_bytes=64, name="scales")
+            xw = x_sb[i][:].bitcast(F32).rearrange("p (c g) -> p g c", g=G)
+            banks = []
             for g in range(G):
-                xt = pst.tile([P, U * P], F32, tag="tr")
+                xt = pst.tile([P, U * P], F32, tag="tr", name="xt")
                 for u in range(U):
                     nc.tensor.transpose(xt[:, u * P:(u + 1) * P], xw[:, g, u * P:(u + 1) * P], ident_f[:])
-                nc.scalar.copy(
-                    out=grp[:, 2 * g:2 * g + 2, :, :],
-                    in_=xt[:].bitcast(BF16).rearrange("p (u m t) -> p t m u", u=U, t=2),
-                )
-            qv = q2_sb[:].rearrange("p (c g) -> p g c", g=G)
-            for g0, ng in ((0, 2), (2, 1)):
-                qt = pst.tile([P, ng * U * P], BF16, tag="tr")
-                for g in range(ng):
-                    for u in range(U):
-                        j = g * U + u
-                        nc.tensor.transpose(qt[:, j * P:(j + 1) * P], qv[:, g0 + g, u * P:(u + 1) * P], ident_b[:])
-                nc.vector.tensor_copy(
-                    out=grp[:, 6 + g0:6 + g0 + ng, :, :],
-                    in_=qt[:].rearrange("p (g u m) -> p g m u", g=ng, u=U),
-                )
-            for p0, npos in ((0, 2), (2, 2), (4, 2), (6, 2), (8, 1)):
-                nc.vector.quantize_mx(
-                    out=codes[:, p0:p0 + npos, :].rearrange("p a m -> p (a m)").bitcast(FP8X4),
-                    scales=scales[:, p0:p0 + npos, :].rearrange("p a m -> p (a m)"),
-                    in_=grp[:, p0:p0 + npos, :, :].rearrange("p a m u -> p (a m u)"),
-                )
+                banks.append(xt)
+            return banks
 
-            acc = res.tile([P, O * G], F32)
-            nc.gpsimd.tensor_tensor(
-                out=acc[:].rearrange("p (o g) -> p o g", g=G),
-                in0=q1_sb[:].rearrange("p (o g) -> p o g", g=G),
+        def ev_x(i, g, xt):
+            nc.scalar.copy(
+                out=grp[i][:, 2 * g:2 * g + 2, :, :],
+                in_=xt[:].bitcast(BF16).rearrange("p (u m t) -> p t m u", u=U, t=2),
+            )
+
+        def tx_q(i):
+            banks = []
+            for g0, ng in ((0, 2), (2, 1)):
+                qt = pst.tile([P, ng * U * P], BF16, tag="tr", name="qt")
+                for g in range(ng):
+                    for b in range(NB):
+                        j = g * NB + b
+                        nc.tensor.transpose(
+                            qt[:, j * P:(j + 1) * P],
+                            q2_sb[i][:, b, :].rearrange("p (c g) -> p g c", g=G)[:, g0 + g, :],
+                            ident_b[:],
+                        )
+                banks.append((g0, ng, qt))
+            return banks
+
+        def ev_q(i, g0, ng, qt):
+            nc.vector.tensor_copy(
+                out=grp[i][:, 6 + g0:6 + g0 + ng, :, :].rearrange("p a m u -> p (a m u)"),
+                in_=qt[:],
+            )
+
+        def quant(i, p0, npos):
+            nc.vector.quantize_mx(
+                out=codes[i][:, p0:p0 + npos, :].rearrange("p a m -> p (a m)").bitcast(FP8X4),
+                scales=scales[i][:, p0:p0 + npos, :].rearrange("p a m -> p (a m)"),
+                in_=grp[i][:, p0:p0 + npos, :, :].rearrange("p a m u -> p (a m u)"),
+            )
+
+        def residual(i):
+            acc[i] = res.tile([P, O * G], F32, name="acc")
+            nc.vector.tensor_tensor(
+                out=acc[i][:].rearrange("p (o g) -> p o g", g=G),
+                in0=q1_sb[i][:].rearrange("p (o g) -> p o g", g=G),
                 in1=b_bc[:].unsqueeze(2).to_broadcast([P, O, G]),
                 op=ADD,
             )
-            for oc in range(OT):
-                ps = psm.tile([P, G, P], F32, tag="mm")
+
+        def mm(i, oc):
+            ps[oc] = psm.tile([P, G, P], F32, tag="mm", name="ps")
+            for g in range(G):
+                for k in range(KW):
+                    pos = 2 * g + k if k < 2 else 6 + g
+                    nc.tensor.matmul_mx(
+                        out=ps[oc][:, g, :],
+                        lhsT=codes[i][:, pos, :].bitcast(FP8X4),
+                        lhsT_scale=scales[i][:, pos, :],
+                        rhs=w_codes[:, k, oc * P:(oc + 1) * P].bitcast(FP8X4),
+                        rhs_scale=w_scales[:, k, oc * P:(oc + 1) * P],
+                        start=(k == 0),
+                        stop=(k == KW - 1),
+                    )
+
+        def add(i, oc):
+            part = acc[i][:, oc * P * G:(oc + 1) * P * G].rearrange("p (o g) -> p o g", g=G)
+            nc.vector.tensor_tensor(out=part, in0=ps[oc][:].rearrange("p g o -> p o g"), in1=part, op=ADD)
+
+        def relu_store(i, h):
+            half = O * G // 2
+            part = acc[i][:, h * half:(h + 1) * half]
+            nc.scalar.activation(out=part, in_=part, func=RELU)
+            nc.scalar.dma_start(out=out_t[i][:, h * half:(h + 1) * half], in_=part)
+
+        w_sb = const.tile([P, 2, 8, P * KW], BF16)
+        for h in range(2):
+            nc.sync.dma_start(out=w_sb[:, h, :, :], in_=w_t[h])
+        b_bc = const.tile([P, O], BF16)
+        nc.scalar.dma_start(out=b_bc[:], in_=b3.partition_broadcast(P))
+        for i in range(AHEAD):
+            load(i)
+        ident_b = const.tile([P, P], BF16)
+        make_identity(nc, ident_b[:])
+        ident_f = const.tile([P, P], F32)
+        make_identity(nc, ident_f[:])
+
+        w_grp = const.tile([P, KW, O * U], BF16, align_bytes=64)
+        w_codes = const.tile([P, KW, O], U32, align_bytes=64)
+        w_scales = const.tile([P, KW, O], U8, align_bytes=64)
+        for h in range(2):
+            for k in range(KW):
+                wt = pst.tile([P, 8 * P], BF16, tag="tr", name="wt")
+                for b in range(8):
+                    nc.tensor.transpose(
+                        wt[:, b * P:(b + 1) * P],
+                        w_sb[:, h, b, :].rearrange("p (c k) -> p k c", k=KW)[:, k, :],
+                        ident_b[:],
+                    )
+                dst = w_grp[:, k, h * 1024:(h + 1) * 1024]
+                if k == 1:
+                    nc.scalar.copy(out=dst, in_=wt[:])
+                else:
+                    nc.vector.tensor_copy(out=dst, in_=wt[:])
+        xb = tx_x(0)
+        for g in range(G):
+            ev_x(0, g, xb[g])
+        for k in range(KW):
+            nc.vector.quantize_mx(
+                out=w_codes[:, k, :].bitcast(FP8X4), scales=w_scales[:, k, :], in_=w_grp[:, k, :]
+            )
+        for g0, ng, qt in tx_q(0):
+            ev_q(0, g0, ng, qt)
+        residual(0)
+        for p0, npos in ((0, 2), (2, 2), (4, 2), (6, 2), (8, 1)):
+            quant(0, p0, npos)
+
+        for i in range(NT):
+            nxt = i + 1
+            more = nxt < NT
+            if i + AHEAD < NT:
+                load(i + AHEAD)
+            if more:
+                xb = tx_x(nxt)
+            if i > 0:
+                add(i - 1, 2)
+                add(i - 1, 3)
+                relu_store(i - 1, 1)
+            if more:
                 for g in range(G):
-                    for k in range(KW):
-                        pos = 2 * g + k if k < 2 else 6 + g
-                        nc.tensor.matmul_mx(
-                            out=ps[:, g, :],
-                            lhsT=codes[:, pos, :].bitcast(FP8X4),
-                            lhsT_scale=scales[:, pos, :],
-                            rhs=w_codes[:, k, oc * P:(oc + 1) * P].bitcast(FP8X4),
-                            rhs_scale=w_scales[:, k, oc * P:(oc + 1) * P],
-                            start=(k == 0),
-                            stop=(k == KW - 1),
-                        )
-                part = acc[:, oc * P * G:(oc + 1) * P * G]
-                nc.vector.tensor_tensor(
-                    out=part.rearrange("p (o g) -> p o g", g=G),
-                    in0=ps[:].rearrange("p g o -> p o g"),
-                    in1=part.rearrange("p (o g) -> p o g", g=G),
-                    op=ADD,
-                )
-            nc.scalar.activation(out=acc[:], in_=acc[:], func=RELU)
-            nc.scalar.dma_start(out=out_t[i], in_=acc[:])
+                    ev_x(nxt, g, xb[g])
+                residual(nxt)
+            mm(i, 0)
+            mm(i, 1)
+            add(i, 0)
+            if more:
+                quant(nxt, 0, 2)
+            add(i, 1)
+            if more:
+                quant(nxt, 2, 2)
+                for g0, ng, qt in tx_q(nxt):
+                    ev_q(nxt, g0, ng, qt)
+                quant(nxt, 4, 2)
+                quant(nxt, 6, 2)
+                quant(nxt, 8, 1)
+            relu_store(i, 0)
+            mm(i, 2)
+            mm(i, 3)
+        add(NT - 1, 2)
+        add(NT - 1, 3)
+        relu_store(NT - 1, 1)

@@ -19,7 +19,7 @@ U = C // P
 OT = O // P
 NB = 4
 NPOS = 9
-AHEAD = 2
+AHEAD = 3
 FLOPS = 2 * N * G * O * C * KW
 
 
@@ -35,7 +35,7 @@ def tile_quadjetresnetblock_pb_t_kernel(tc, x, q2, q1, W3, b3, out):
         const = ctx.enter_context(tc.tile_pool(name="const", bufs=1))
         xin = ctx.enter_context(tc.tile_pool(name="xin", bufs=AHEAD + 2))
         work = ctx.enter_context(tc.tile_pool(name="work", bufs=2))
-        res = ctx.enter_context(tc.tile_pool(name="res", bufs=4))
+        res = ctx.enter_context(tc.tile_pool(name="res", bufs=6))
         pst = ctx.enter_context(tc.psum_pool(name="pst", bufs=4))
         psm = ctx.enter_context(tc.psum_pool(name="psm", bufs=4))
         ctx.enter_context(tc.manual_schedule())
@@ -99,12 +99,14 @@ def tile_quadjetresnetblock_pb_t_kernel(tc, x, q2, q1, W3, b3, out):
 
         def residual(i):
             acc[i] = res.tile([P, O * G], F32, name="acc")
-            nc.vector.tensor_tensor(
-                out=acc[i][:].rearrange("p (o g) -> p o g", g=G),
-                in0=q1_sb[i][:].rearrange("p (o g) -> p o g", g=G),
-                in1=b_bc[:].unsqueeze(2).to_broadcast([P, O, G]),
-                op=ADD,
-            )
+            for oc in range(OT):
+                cols = slice(oc * P * G, (oc + 1) * P * G)
+                nc.gpsimd.tensor_tensor(
+                    out=acc[i][:, cols].rearrange("p (o g) -> p o g", g=G),
+                    in0=q1_sb[i][:, cols].rearrange("p (o g) -> p o g", g=G),
+                    in1=b_bc[:, oc * P:(oc + 1) * P].unsqueeze(2).to_broadcast([P, P, G]),
+                    op=ADD,
+                )
 
         def mm(i, oc):
             ps[oc] = psm.tile([P, G, P], F32, tag="mm", name="ps")
@@ -125,11 +127,10 @@ def tile_quadjetresnetblock_pb_t_kernel(tc, x, q2, q1, W3, b3, out):
             part = acc[i][:, oc * P * G:(oc + 1) * P * G].rearrange("p (o g) -> p o g", g=G)
             nc.vector.tensor_tensor(out=part, in0=ps[oc][:].rearrange("p g o -> p o g"), in1=part, op=ADD)
 
-        def relu_store(i, h):
-            half = O * G // 2
-            part = acc[i][:, h * half:(h + 1) * half]
+        def relu_store(i, lo, hi):
+            part = acc[i][:, lo:hi]
             nc.scalar.activation(out=part, in_=part, func=RELU)
-            nc.scalar.dma_start(out=out_t[i][:, h * half:(h + 1) * half], in_=part)
+            nc.scalar.dma_start(out=out_t[i][:, lo:hi], in_=part)
 
         w_sb = const.tile([P, 2, 8, P * KW], BF16)
         for h in range(2):
@@ -170,40 +171,40 @@ def tile_quadjetresnetblock_pb_t_kernel(tc, x, q2, q1, W3, b3, out):
         for g0, ng, qt in tx_q(0):
             ev_q(0, g0, ng, qt)
         residual(0)
-        for p0, npos in ((0, 2), (2, 2), (4, 2), (6, 2), (8, 1)):
+        residual(1)
+        for p0, npos in ((0, 4), (4, 4), (8, 1)):
             quant(0, p0, npos)
 
+        half = O * G // 2
         for i in range(NT):
             nxt = i + 1
             more = nxt < NT
             if i + AHEAD < NT:
                 load(i + AHEAD)
+            if i + 2 < NT:
+                residual(i + 2)
             if more:
                 xb = tx_x(nxt)
+                for g in range(G):
+                    ev_x(nxt, g, xb[g])
             if i > 0:
                 add(i - 1, 2)
                 add(i - 1, 3)
-                relu_store(i - 1, 1)
-            if more:
-                for g in range(G):
-                    ev_x(nxt, g, xb[g])
-                residual(nxt)
+                relu_store(i - 1, 0, O * G)
             mm(i, 0)
             mm(i, 1)
             add(i, 0)
             if more:
-                quant(nxt, 0, 2)
+                quant(nxt, 0, 4)
             add(i, 1)
             if more:
-                quant(nxt, 2, 2)
                 for g0, ng, qt in tx_q(nxt):
                     ev_q(nxt, g0, ng, qt)
-                quant(nxt, 4, 2)
-                quant(nxt, 6, 2)
+                quant(nxt, 4, 4)
                 quant(nxt, 8, 1)
-            relu_store(i, 0)
             mm(i, 2)
             mm(i, 3)
+        relu_store(NT - 1, 0, half)
         add(NT - 1, 2)
         add(NT - 1, 3)
-        relu_store(NT - 1, 1)
+        relu_store(NT - 1, half, O * G)

@@ -15,26 +15,27 @@ P = 128
 N, C, G, KW = 1536, 512, 3, 3
 O = 512
 NT = N // P
-U = C // P
+PACK = 4
 OT = O // P
-NB = 4
+HB = 64
 NPOS = 9
-AHEAD = 3
+LAG = 2
+AHEAD = 4
 FLOPS = 2 * N * G * O * C * KW
 
 
 def tile_quadjetresnetblock_pb_t_kernel(tc, x, q2, q1, W3, b3, out):
     nc = tc.nc
     x_t = x.rearrange("(i p) c j -> i p (c j)", p=P)
-    q2_t = q2.rearrange("n (u c) g -> (n u) (c g)", u=U).rearrange("(i b p) f -> i p b f", b=NB, p=P)
+    q2_t = q2.rearrange("n (h c) g -> (n h) (c g)", h=2).rearrange("(i b p) f -> i p b f", b=2, p=P)
     q1_t = q1.rearrange("(i p) c g -> i p (c g)", p=P)
     out_t = out.rearrange("(i p) o g -> i p (o g)", p=P)
-    w_t = W3.rearrange("o (u c) k -> (o u) (c k)", u=U).rearrange("(h b p) f -> h p b f", h=2, p=P)
+    w_t = W3.rearrange("o (h c) k -> (o h) (c k)", h=2).rearrange("(d b p) f -> d p b f", b=2, p=P)
 
     with ExitStack() as ctx:
         const = ctx.enter_context(tc.tile_pool(name="const", bufs=1))
         xin = ctx.enter_context(tc.tile_pool(name="xin", bufs=AHEAD + 2))
-        work = ctx.enter_context(tc.tile_pool(name="work", bufs=2))
+        work = ctx.enter_context(tc.tile_pool(name="work", bufs=LAG + 1))
         res = ctx.enter_context(tc.tile_pool(name="res", bufs=6))
         pst = ctx.enter_context(tc.psum_pool(name="pst", bufs=4))
         psm = ctx.enter_context(tc.psum_pool(name="psm", bufs=4))
@@ -42,53 +43,55 @@ def tile_quadjetresnetblock_pb_t_kernel(tc, x, q2, q1, W3, b3, out):
 
         x_sb, q2_sb, q1_sb, grp, codes, scales, acc, ps = {}, {}, {}, {}, {}, {}, {}, {}
 
-        def load(i):
+        def load_xq(i):
             x_sb[i] = xin.tile([P, C * 6], BF16, name="x_sb")
             nc.sync.dma_start(out=x_sb[i][:], in_=x_t[i])
-            q2_sb[i] = xin.tile([P, NB, P * G], BF16, name="q2_sb")
+            q2_sb[i] = xin.tile([P, 2, C * G // 2], BF16, name="q2_sb")
             nc.sync.dma_start(out=q2_sb[i][:], in_=q2_t[i])
+
+        def load_q1(i):
             q1_sb[i] = xin.tile([P, C * G], BF16, name="q1_sb")
             nc.sync.dma_start(out=q1_sb[i][:], in_=q1_t[i])
 
         def tx_x(i):
-            grp[i] = work.tile([P, NPOS, P, U], BF16, align_bytes=64, name="grp")
+            grp[i] = work.tile([P, NPOS, P, PACK], BF16, align_bytes=64, name="grp")
             codes[i] = work.tile([P, NPOS, P], U32, align_bytes=64, name="codes")
             scales[i] = work.tile([P, NPOS, P], U8, align_bytes=64, name="scales")
-            xw = x_sb[i][:].bitcast(F32).rearrange("p (c g) -> p g c", g=G)
+            xw = x_sb[i][:].bitcast(F32).rearrange("p (h i e g) -> p h e g i", h=2, e=2, g=G)
             banks = []
             for g in range(G):
-                xt = pst.tile([P, U * P], F32, tag="tr", name="xt")
-                for u in range(U):
-                    nc.tensor.transpose(xt[:, u * P:(u + 1) * P], xw[:, g, u * P:(u + 1) * P], ident_f[:])
+                xt = pst.tile([P, PACK * P], F32, tag="tr", name="xt")
+                for t in range(PACK):
+                    nc.tensor.transpose(xt[:, t * P:(t + 1) * P], xw[:, t // 2, t % 2, g, :], ident_f[:])
                 banks.append(xt)
             return banks
 
         def ev_x(i, g, xt):
             nc.scalar.copy(
                 out=grp[i][:, 2 * g:2 * g + 2, :, :],
-                in_=xt[:].bitcast(BF16).rearrange("p (u m t) -> p t m u", u=U, t=2),
+                in_=xt[:].bitcast(BF16).rearrange("p (t m k) -> p k m t", t=PACK, k=2),
             )
 
-        def tx_q(i):
-            banks = []
-            for g0, ng in ((0, 2), (2, 1)):
-                qt = pst.tile([P, ng * U * P], BF16, tag="tr", name="qt")
-                for g in range(ng):
-                    for b in range(NB):
-                        j = g * NB + b
-                        nc.tensor.transpose(
-                            qt[:, j * P:(j + 1) * P],
-                            q2_sb[i][:, b, :].rearrange("p (c g) -> p g c", g=G)[:, g0 + g, :],
-                            ident_b[:],
-                        )
-                banks.append((g0, ng, qt))
-            return banks
+        def tx_triples(rows):
+            words = rows.bitcast(F32).rearrange("p (i r) -> p r i", r=3)
+            bank = pst.tile([P, PACK * P], F32, tag="tr", name="bank")
+            for r in range(3):
+                nc.tensor.transpose(bank[:, r * P:(r + 1) * P], words[:, r, :], ident_f[:])
+            return bank
 
-        def ev_q(i, g0, ng, qt):
-            nc.vector.tensor_copy(
-                out=grp[i][:, 6 + g0:6 + g0 + ng, :, :].rearrange("p a m u -> p (a m u)"),
-                in_=qt[:],
-            )
+        def pick(bank, s):
+            off = [256 * ((3 * e + s) // 2) + (3 * e + s) % 2 for e in range(2)]
+            step = off[1] - off[0]
+            flat = bank[:].bitcast(BF16)[:, off[0]:off[0] + 2 * step]
+            cols = flat.rearrange("p (e b) -> p e b", e=2)[:, :, 0:2 * P]
+            return cols.rearrange("p e (j s) -> p j e s", s=2)[:, :, :, 0]
+
+        def ev_q(i, b, bank):
+            for g in range(G):
+                nc.vector.tensor_copy(
+                    out=grp[i][:, 6 + g, b * HB:(b + 1) * HB, :].rearrange("p n (h e) -> p (n h) e", e=2),
+                    in_=pick(bank, g),
+                )
 
         def quant(i, p0, npos):
             nc.vector.quantize_mx(
@@ -127,70 +130,75 @@ def tile_quadjetresnetblock_pb_t_kernel(tc, x, q2, q1, W3, b3, out):
             part = acc[i][:, oc * P * G:(oc + 1) * P * G].rearrange("p (o g) -> p o g", g=G)
             nc.vector.tensor_tensor(out=part, in0=ps[oc][:].rearrange("p g o -> p o g"), in1=part, op=ADD)
 
-        def relu_store(i, lo, hi):
+        def relu_store(i, oc0, oc1):
+            lo, hi = oc0 * P * G, oc1 * P * G
             part = acc[i][:, lo:hi]
             nc.scalar.activation(out=part, in_=part, func=RELU)
             nc.scalar.dma_start(out=out_t[i][:, lo:hi], in_=part)
 
-        w_sb = const.tile([P, 2, 8, P * KW], BF16)
-        for h in range(2):
-            nc.sync.dma_start(out=w_sb[:, h, :, :], in_=w_t[h])
+        def prepare(i):
+            xb = tx_x(i)
+            for g in range(G):
+                ev_x(i, g, xb[g])
+            quant(i, 0, 4)
+            for b in range(2):
+                ev_q(i, b, tx_triples(q2_sb[i][:, b, :]))
+            quant(i, 4, 4)
+            quant(i, 8, 1)
+
+        w_sb = const.tile([P, 4, 2, C * KW // 2], BF16)
+        for d in range(4):
+            nc.sync.dma_start(out=w_sb[:, d, :, :], in_=w_t[d])
         b_bc = const.tile([P, O], BF16)
         nc.scalar.dma_start(out=b_bc[:], in_=b3.partition_broadcast(P))
-        for i in range(AHEAD):
-            load(i)
-        ident_b = const.tile([P, P], BF16)
-        make_identity(nc, ident_b[:])
+        for i in range(LAG):
+            load_xq(i)
+        for i in range(LAG):
+            load_q1(i)
+        for i in range(LAG, AHEAD):
+            load_xq(i)
+            load_q1(i)
         ident_f = const.tile([P, P], F32)
         make_identity(nc, ident_f[:])
 
-        w_grp = const.tile([P, KW, O * U], BF16, align_bytes=64)
+        w_grp = const.tile([P, KW, O, PACK], BF16, align_bytes=64)
         w_codes = const.tile([P, KW, O], U32, align_bytes=64)
         w_scales = const.tile([P, KW, O], U8, align_bytes=64)
-        for h in range(2):
-            for k in range(KW):
-                wt = pst.tile([P, 8 * P], BF16, tag="tr", name="wt")
-                for b in range(8):
-                    nc.tensor.transpose(
-                        wt[:, b * P:(b + 1) * P],
-                        w_sb[:, h, b, :].rearrange("p (c k) -> p k c", k=KW)[:, k, :],
-                        ident_b[:],
-                    )
-                dst = w_grp[:, k, h * 1024:(h + 1) * 1024]
-                if k == 1:
-                    nc.scalar.copy(out=dst, in_=wt[:])
-                else:
-                    nc.vector.tensor_copy(out=dst, in_=wt[:])
-        xb = tx_x(0)
-        for g in range(G):
-            ev_x(0, g, xb[g])
+        for d in range(4):
+            for b in range(2):
+                bank = tx_triples(w_sb[:, d, b, :])
+                o0 = (2 * d + b) * HB
+                for k in range(KW):
+                    dst = w_grp[:, k, o0:o0 + HB, :].rearrange("p n (h e) -> p (n h) e", e=2)
+                    if b == 0:
+                        nc.vector.tensor_copy(out=dst, in_=pick(bank, k))
+                    else:
+                        nc.scalar.copy(out=dst, in_=pick(bank, k))
         for k in range(KW):
             nc.vector.quantize_mx(
-                out=w_codes[:, k, :].bitcast(FP8X4), scales=w_scales[:, k, :], in_=w_grp[:, k, :]
+                out=w_codes[:, k, :].bitcast(FP8X4),
+                scales=w_scales[:, k, :],
+                in_=w_grp[:, k, :, :].rearrange("p o u -> p (o u)"),
             )
-        for g0, ng, qt in tx_q(0):
-            ev_q(0, g0, ng, qt)
-        residual(0)
-        residual(1)
-        for p0, npos in ((0, 4), (4, 4), (8, 1)):
-            quant(0, p0, npos)
+        for i in range(LAG):
+            prepare(i)
+            residual(i)
 
-        half = O * G // 2
         for i in range(NT):
-            nxt = i + 1
+            nxt = i + LAG
             more = nxt < NT
             if i + AHEAD < NT:
-                load(i + AHEAD)
-            if i + 2 < NT:
-                residual(i + 2)
+                load_xq(i + AHEAD)
+                load_q1(i + AHEAD)
             if more:
+                residual(nxt)
                 xb = tx_x(nxt)
                 for g in range(G):
                     ev_x(nxt, g, xb[g])
             if i > 0:
                 add(i - 1, 2)
                 add(i - 1, 3)
-                relu_store(i - 1, 0, O * G)
+                relu_store(i - 1, 0, OT)
             mm(i, 0)
             mm(i, 1)
             add(i, 0)
@@ -198,13 +206,14 @@ def tile_quadjetresnetblock_pb_t_kernel(tc, x, q2, q1, W3, b3, out):
                 quant(nxt, 0, 4)
             add(i, 1)
             if more:
-                for g0, ng, qt in tx_q(nxt):
-                    ev_q(nxt, g0, ng, qt)
+                for b in range(2):
+                    ev_q(nxt, b, tx_triples(q2_sb[nxt][:, b, :]))
                 quant(nxt, 4, 4)
                 quant(nxt, 8, 1)
             mm(i, 2)
             mm(i, 3)
-        relu_store(NT - 1, 0, half)
+        relu_store(NT - 1, 0, 2)
         add(NT - 1, 2)
+        relu_store(NT - 1, 2, 3)
         add(NT - 1, 3)
-        relu_store(NT - 1, half, O * G)
+        relu_store(NT - 1, 3, 4)

@@ -26,7 +26,7 @@ FLOPS = 2 * N * G * O * C * KW
 
 def tile_quadjetresnetblock_pb_t_kernel(tc, x, q2, q1, W3, b3, out):
     nc = tc.nc
-    x_t = x.rearrange("(i p) c j -> i p (c j)", p=P)
+    x_t = x.rearrange("n (h c) j -> (n h) (c j)", h=2).rearrange("(i b p) f -> i p b f", b=2, p=P)
     q2_t = q2.rearrange("n (h c) g -> (n h) (c g)", h=2).rearrange("(i b p) f -> i p b f", b=2, p=P)
     q1_t = q1.rearrange("(i p) c g -> i p (c g)", p=P)
     out_t = out.rearrange("(i p) o g -> i p (o g)", p=P)
@@ -44,7 +44,7 @@ def tile_quadjetresnetblock_pb_t_kernel(tc, x, q2, q1, W3, b3, out):
         x_sb, q2_sb, q1_sb, grp, codes, scales, acc, ps = {}, {}, {}, {}, {}, {}, {}, {}
 
         def load_xq(i):
-            x_sb[i] = xin.tile([P, C * 6], BF16, name="x_sb")
+            x_sb[i] = xin.tile([P, 2, C * 6 // 2], BF16, name="x_sb")
             nc.sync.dma_start(out=x_sb[i][:], in_=x_t[i])
             q2_sb[i] = xin.tile([P, 2, C * G // 2], BF16, name="q2_sb")
             nc.sync.dma_start(out=q2_sb[i][:], in_=q2_t[i])
@@ -57,19 +57,21 @@ def tile_quadjetresnetblock_pb_t_kernel(tc, x, q2, q1, W3, b3, out):
             grp[i] = work.tile([P, NPOS, P, PACK], BF16, align_bytes=64, name="grp")
             codes[i] = work.tile([P, NPOS, P], U32, align_bytes=64, name="codes")
             scales[i] = work.tile([P, NPOS, P], U8, align_bytes=64, name="scales")
-            xw = x_sb[i][:].bitcast(F32).rearrange("p (h i e g) -> p h e g i", h=2, e=2, g=G)
             banks = []
             for g in range(G):
                 xt = pst.tile([P, PACK * P], F32, tag="tr", name="xt")
-                for t in range(PACK):
-                    nc.tensor.transpose(xt[:, t * P:(t + 1) * P], xw[:, t // 2, t % 2, g, :], ident_f[:])
+                for e in range(2):
+                    for b in range(2):
+                        xw = x_sb[i][:, b, :].bitcast(F32).rearrange("p (i e g) -> p e g i", e=2, g=G)
+                        j = 2 * e + b
+                        nc.tensor.transpose(xt[:, j * P:(j + 1) * P], xw[:, e, g, :], ident_f[:])
                 banks.append(xt)
             return banks
 
         def ev_x(i, g, xt):
             nc.scalar.copy(
-                out=grp[i][:, 2 * g:2 * g + 2, :, :],
-                in_=xt[:].bitcast(BF16).rearrange("p (t m k) -> p k m t", t=PACK, k=2),
+                out=grp[i][:, 2 * g:2 * g + 2, :, :].rearrange("p k m (h e) -> p k (m h) e", e=2),
+                in_=xt[:].bitcast(BF16).rearrange("p (e j k) -> p k j e", e=2, k=2),
             )
 
         def tx_triples(rows):

@@ -21,12 +21,13 @@ HB = 64
 NPOS = 9
 LAG = 2
 AHEAD = 4
+OC_POOL = 3
 FLOPS = 2 * N * G * O * C * KW
 
 
 def tile_quadjetresnetblock_pb_t_kernel(tc, x, q2, q1, W3, b3, out):
     nc = tc.nc
-    x_t = x.rearrange("n (h c) j -> (n h) (c j)", h=2).rearrange("(i b p) f -> i p b f", b=2, p=P)
+    x_t = x.rearrange("(i p) c j -> i p (c j)", p=P)
     q2_t = q2.rearrange("n (h c) g -> (n h) (c g)", h=2).rearrange("(i b p) f -> i p b f", b=2, p=P)
     q1_t = q1.rearrange("(i p) c g -> i p (c g)", p=P)
     out_t = out.rearrange("(i p) o g -> i p (o g)", p=P)
@@ -44,7 +45,7 @@ def tile_quadjetresnetblock_pb_t_kernel(tc, x, q2, q1, W3, b3, out):
         x_sb, q2_sb, q1_sb, grp, codes, scales, acc, ps = {}, {}, {}, {}, {}, {}, {}, {}
 
         def load_xq(i):
-            x_sb[i] = xin.tile([P, 2, C * 6 // 2], BF16, name="x_sb")
+            x_sb[i] = xin.tile([P, C * 6], BF16, name="x_sb")
             nc.sync.dma_start(out=x_sb[i][:], in_=x_t[i])
             q2_sb[i] = xin.tile([P, 2, C * G // 2], BF16, name="q2_sb")
             nc.sync.dma_start(out=q2_sb[i][:], in_=q2_t[i])
@@ -57,21 +58,19 @@ def tile_quadjetresnetblock_pb_t_kernel(tc, x, q2, q1, W3, b3, out):
             grp[i] = work.tile([P, NPOS, P, PACK], BF16, align_bytes=64, name="grp")
             codes[i] = work.tile([P, NPOS, P], U32, align_bytes=64, name="codes")
             scales[i] = work.tile([P, NPOS, P], U8, align_bytes=64, name="scales")
+            xw = x_sb[i][:].bitcast(F32).rearrange("p (h i e g) -> p h e g i", h=2, e=2, g=G)
             banks = []
             for g in range(G):
                 xt = pst.tile([P, PACK * P], F32, tag="tr", name="xt")
-                for e in range(2):
-                    for b in range(2):
-                        xw = x_sb[i][:, b, :].bitcast(F32).rearrange("p (i e g) -> p e g i", e=2, g=G)
-                        j = 2 * e + b
-                        nc.tensor.transpose(xt[:, j * P:(j + 1) * P], xw[:, e, g, :], ident_f[:])
+                for t in range(PACK):
+                    nc.tensor.transpose(xt[:, t * P:(t + 1) * P], xw[:, t // 2, t % 2, g, :], ident_f[:])
                 banks.append(xt)
             return banks
 
         def ev_x(i, g, xt):
             nc.scalar.copy(
-                out=grp[i][:, 2 * g:2 * g + 2, :, :].rearrange("p k m (h e) -> p k (m h) e", e=2),
-                in_=xt[:].bitcast(BF16).rearrange("p (e j k) -> p k j e", e=2, k=2),
+                out=grp[i][:, 2 * g:2 * g + 2, :, :],
+                in_=xt[:].bitcast(BF16).rearrange("p (t m k) -> p k m t", t=PACK, k=2),
             )
 
         def tx_triples(rows):
@@ -102,16 +101,19 @@ def tile_quadjetresnetblock_pb_t_kernel(tc, x, q2, q1, W3, b3, out):
                 in_=grp[i][:, p0:p0 + npos, :, :].rearrange("p a m u -> p (a m u)"),
             )
 
+        def residual_part(engine, i, oc):
+            cols = slice(oc * P * G, (oc + 1) * P * G)
+            engine.tensor_tensor(
+                out=acc[i][:, cols].rearrange("p (o g) -> p o g", g=G),
+                in0=q1_sb[i][:, cols].rearrange("p (o g) -> p o g", g=G),
+                in1=b_bc[:, oc * P:(oc + 1) * P].unsqueeze(2).to_broadcast([P, P, G]),
+                op=ADD,
+            )
+
         def residual(i):
             acc[i] = res.tile([P, O * G], F32, name="acc")
             for oc in range(OT):
-                cols = slice(oc * P * G, (oc + 1) * P * G)
-                nc.gpsimd.tensor_tensor(
-                    out=acc[i][:, cols].rearrange("p (o g) -> p o g", g=G),
-                    in0=q1_sb[i][:, cols].rearrange("p (o g) -> p o g", g=G),
-                    in1=b_bc[:, oc * P:(oc + 1) * P].unsqueeze(2).to_broadcast([P, P, G]),
-                    op=ADD,
-                )
+                residual_part(nc.gpsimd if oc < OC_POOL else nc.vector, i, oc)
 
         def mm(i, oc):
             ps[oc] = psm.tile([P, G, P], F32, tag="mm", name="ps")

from contextlib import ExitStack

import concourse.mybir as mybir
from concourse.masks import make_identity

F32 = mybir.dt.float32
BF16 = mybir.dt.bfloat16
U32 = mybir.dt.uint32
U8 = mybir.dt.uint8
FP8X4 = mybir.dt.float8_e4m3fn_x4
ADD = mybir.AluOpType.add
RELU = mybir.ActivationFunctionType.Relu

P = 128
N, C, G, KW = 1536, 512, 3, 3
O = 512
NT = N // P
PACK = 4
OT = O // P
HB = 64
NPOS = 9
LAG = 2
AHEAD = 4
OC_POOL = 3
FLOPS = 2 * N * G * O * C * KW


def tile_quadjetresnetblock_pb_t_kernel(tc, x, q2, q1, W3, b3, out):
    nc = tc.nc
    x_t = x.rearrange("(i p) c j -> i p (c j)", p=P)
    q2_t = q2.rearrange("n (h c) g -> (n h) (c g)", h=2).rearrange("(i b p) f -> i p b f", b=2, p=P)
    q1_t = q1.rearrange("(i p) c g -> i p (c g)", p=P)
    out_t = out.rearrange("(i p) o g -> i p (o g)", p=P)
    w_t = W3.rearrange("o (h c) k -> (o h) (c k)", h=2).rearrange("(d b p) f -> d p b f", b=2, p=P)

    with ExitStack() as ctx:
        const = ctx.enter_context(tc.tile_pool(name="const", bufs=1))
        xin = ctx.enter_context(tc.tile_pool(name="xin", bufs=AHEAD + 2))
        work = ctx.enter_context(tc.tile_pool(name="work", bufs=LAG + 1))
        res = ctx.enter_context(tc.tile_pool(name="res", bufs=6))
        pst = ctx.enter_context(tc.psum_pool(name="pst", bufs=4))
        psm = ctx.enter_context(tc.psum_pool(name="psm", bufs=4))
        ctx.enter_context(tc.manual_schedule())

        x_sb, q2_sb, q1_sb, grp, codes, scales, acc, ps = {}, {}, {}, {}, {}, {}, {}, {}

        def load_xq(i):
            x_sb[i] = xin.tile([P, C * 6], BF16, name="x_sb")
            nc.sync.dma_start(out=x_sb[i][:], in_=x_t[i])
            q2_sb[i] = xin.tile([P, 2, C * G // 2], BF16, name="q2_sb")
            nc.sync.dma_start(out=q2_sb[i][:], in_=q2_t[i])

        def load_q1(i):
            q1_sb[i] = xin.tile([P, C * G], BF16, name="q1_sb")
            nc.sync.dma_start(out=q1_sb[i][:], in_=q1_t[i])

        def tx_x(i):
            grp[i] = work.tile([P, NPOS, P, PACK], BF16, align_bytes=64, name="grp")
            codes[i] = work.tile([P, NPOS, P], U32, align_bytes=64, name="codes")
            scales[i] = work.tile([P, NPOS, P], U8, align_bytes=64, name="scales")
            xw = x_sb[i][:].bitcast(F32).rearrange("p (h i e g) -> p h e g i", h=2, e=2, g=G)
            banks = []
            for g in range(G):
                xt = pst.tile([P, PACK * P], F32, tag="tr", name="xt")
                for t in range(PACK):
                    nc.tensor.transpose(xt[:, t * P:(t + 1) * P], xw[:, t // 2, t % 2, g, :], ident_f[:])
                banks.append(xt)
            return banks

        def ev_x(i, g, xt):
            nc.scalar.copy(
                out=grp[i][:, 2 * g:2 * g + 2, :, :],
                in_=xt[:].bitcast(BF16).rearrange("p (t m k) -> p k m t", t=PACK, k=2),
            )

        def tx_triples(rows):
            words = rows.bitcast(F32).rearrange("p (i r) -> p r i", r=3)
            bank = pst.tile([P, PACK * P], F32, tag="tr", name="bank")
            for r in range(3):
                nc.tensor.transpose(bank[:, r * P:(r + 1) * P], words[:, r, :], ident_f[:])
            return bank

        def pick(bank, s):
            off = [256 * ((3 * e + s) // 2) + (3 * e + s) % 2 for e in range(2)]
            step = off[1] - off[0]
            flat = bank[:].bitcast(BF16)[:, off[0]:off[0] + 2 * step]
            cols = flat.rearrange("p (e b) -> p e b", e=2)[:, :, 0:2 * P]
            return cols.rearrange("p e (j s) -> p j e s", s=2)[:, :, :, 0]

        def ev_q(i, b, bank):
            for g in range(G):
                nc.vector.tensor_copy(
                    out=grp[i][:, 6 + g, b * HB:(b + 1) * HB, :].rearrange("p n (h e) -> p (n h) e", e=2),
                    in_=pick(bank, g),
                )

        def quant(i, p0, npos):
            nc.vector.quantize_mx(
                out=codes[i][:, p0:p0 + npos, :].rearrange("p a m -> p (a m)").bitcast(FP8X4),
                scales=scales[i][:, p0:p0 + npos, :].rearrange("p a m -> p (a m)"),
                in_=grp[i][:, p0:p0 + npos, :, :].rearrange("p a m u -> p (a m u)"),
            )

        def residual_part(engine, i, oc):
            cols = slice(oc * P * G, (oc + 1) * P * G)
            engine.tensor_tensor(
                out=acc[i][:, cols].rearrange("p (o g) -> p o g", g=G),
                in0=q1_sb[i][:, cols].rearrange("p (o g) -> p o g", g=G),
                in1=b_bc[:, oc * P:(oc + 1) * P].unsqueeze(2).to_broadcast([P, P, G]),
                op=ADD,
            )

        def residual(i):
            acc[i] = res.tile([P, O * G], F32, name="acc")
            for oc in range(OT):
                residual_part(nc.gpsimd if oc < OC_POOL else nc.vector, i, oc)

        def mm(i, oc):
            ps[oc] = psm.tile([P, G, P], F32, tag="mm", name="ps")
            for g in range(G):
                for k in range(KW):
                    pos = 2 * g + k if k < 2 else 6 + g
                    nc.tensor.matmul_mx(
                        out=ps[oc][:, g, :],
                        lhsT=codes[i][:, pos, :].bitcast(FP8X4),
                        lhsT_scale=scales[i][:, pos, :],
                        rhs=w_codes[:, k, oc * P:(oc + 1) * P].bitcast(FP8X4),
                        rhs_scale=w_scales[:, k, oc * P:(oc + 1) * P],
                        start=(k == 0),
                        stop=(k == KW - 1),
                    )

        def add(i, oc):
            part = acc[i][:, oc * P * G:(oc + 1) * P * G].rearrange("p (o g) -> p o g", g=G)
            nc.vector.tensor_tensor(out=part, in0=ps[oc][:].rearrange("p g o -> p o g"), in1=part, op=ADD)

        def relu_store(i, oc0, oc1):
            lo, hi = oc0 * P * G, oc1 * P * G
            part = acc[i][:, lo:hi]
            nc.scalar.activation(out=part, in_=part, func=RELU)
            nc.scalar.dma_start(out=out_t[i][:, lo:hi], in_=part)

        def prepare(i):
            xb = tx_x(i)
            for g in range(G):
                ev_x(i, g, xb[g])
            quant(i, 0, 4)
            for b in range(2):
                ev_q(i, b, tx_triples(q2_sb[i][:, b, :]))
            quant(i, 4, 4)
            quant(i, 8, 1)

        w_sb = const.tile([P, 4, 2, C * KW // 2], BF16)
        for d in range(4):
            nc.sync.dma_start(out=w_sb[:, d, :, :], in_=w_t[d])
        b_bc = const.tile([P, O], BF16)
        nc.scalar.dma_start(out=b_bc[:], in_=b3.partition_broadcast(P))
        for i in range(LAG):
            load_xq(i)
        for i in range(LAG):
            load_q1(i)
        for i in range(LAG, AHEAD):
            load_xq(i)
            load_q1(i)
        ident_f = const.tile([P, P], F32)
        make_identity(nc, ident_f[:])

        w_grp = const.tile([P, KW, O, PACK], BF16, align_bytes=64)
        w_codes = const.tile([P, KW, O], U32, align_bytes=64)
        w_scales = const.tile([P, KW, O], U8, align_bytes=64)
        for d in range(4):
            for b in range(2):
                bank = tx_triples(w_sb[:, d, b, :])
                o0 = (2 * d + b) * HB
                for k in range(KW):
                    dst = w_grp[:, k, o0:o0 + HB, :].rearrange("p n (h e) -> p (n h) e", e=2)
                    if b == 0:
                        nc.vector.tensor_copy(out=dst, in_=pick(bank, k))
                    else:
                        nc.scalar.copy(out=dst, in_=pick(bank, k))
        for k in range(KW):
            nc.vector.quantize_mx(
                out=w_codes[:, k, :].bitcast(FP8X4),
                scales=w_scales[:, k, :],
                in_=w_grp[:, k, :, :].rearrange("p o u -> p (o u)"),
            )
        for i in range(LAG):
            prepare(i)
            residual(i)

        for i in range(NT):
            nxt = i + LAG
            more = nxt < NT
            if i + AHEAD < NT:
                load_xq(i + AHEAD)
                load_q1(i + AHEAD)
            if more:
                residual(nxt)
                xb = tx_x(nxt)
                for g in range(G):
                    ev_x(nxt, g, xb[g])
            if i > 0:
                add(i - 1, 2)
                add(i - 1, 3)
                relu_store(i - 1, 0, OT)
            mm(i, 0)
            mm(i, 1)
            add(i, 0)
            if more:
                quant(nxt, 0, 4)
            add(i, 1)
            if more:
                for b in range(2):
                    ev_q(nxt, b, tx_triples(q2_sb[nxt][:, b, :]))
                quant(nxt, 4, 4)
                quant(nxt, 8, 1)
            mm(i, 2)
            mm(i, 3)
        relu_store(NT - 1, 0, 2)
        add(NT - 1, 2)
        relu_store(NT - 1, 2, 3)
        add(NT - 1, 3)
        relu_store(NT - 1, 3, 4)
